import numpy as np
import ml_dtypes

BF16 = ml_dtypes.bfloat16


def bf(x):
    return np.asarray(x, np.float32).astype(BF16)


def f32(x):
    return np.asarray(x, np.float32)


def f64(x):
    return np.asarray(x).astype(np.float64)


def striped(idx):
    return np.tile(idx.reshape(-1, 16).T, (8, 1))


S, D, M, K, E, N = 2048, 128, 128, 128, 128, 1024
TEMP = 0.25


def setup_inputs():
    return {
        "table": bf(np.random.standard_normal((S, D))),
        "wq": bf(np.random.standard_normal((D, M)) / np.sqrt(D)),
        "bq": f32(0.1 * np.random.standard_normal((M, 1))),
        "keys": bf(np.random.standard_normal((M, K)) / (TEMP * np.sqrt(M))),
        "vals": bf(3.0 * np.random.standard_normal((K, E))),
        "bo": f32(0.1 * np.random.standard_normal((E, 1))),
        "probs": f32(np.random.uniform(0.0, 1.0, (1, N))),
        "offs": striped(np.random.permutation(S)[:N]),
    }


def reference(table, wq, bq, keys, vals, bo, probs, offs):
    idx = offs[:16].T.reshape(-1)
    q = f64(wq).T @ f64(table)[idx].T + f64(bq)
    sc = TEMP * (f64(keys).T @ q)
    ex = np.exp(sc - sc.max(axis=0, keepdims=True))
    att = ex / ex.sum(axis=0, keepdims=True)
    return (f64(vals).T @ att + f64(bo)) * f64(probs)

@@ -1,0 +1,110 @@
+import concourse.mybir as mybir
+from concourse.masks import make_identity
+
+BF16, F32, U16 = mybir.dt.bfloat16, mybir.dt.float32, mybir.dt.uint16
+ACT = mybir.ActivationFunctionType
+ALU = mybir.AluOpType
+
+P = 128
+S = 2048
+N = 1024
+PIECE = 512
+BLOCKS = PIECE // P
+CHUNKS = S // PIECE
+TEMP = 0.25
+
+FLOPS = 3 * 2 * P * P * N
+BYTES = N * P * 2 + 3 * P * P * 2 + 2 * P * 4 + N * 4 + P * (N // 16) * 2 + P * N * 4
+
+
+def tile_model_kernel(tc, table, wq, bq, keys, vals, bo, probs, offs, out):
+    nc = tc.nc
+    with (
+        tc.tile_pool(name="held", bufs=1) as held,
+        tc.tile_pool(name="work", bufs=2) as work,
+        tc.psum_pool(name="psum", bufs=2) as psum,
+    ):
+        offsets = held.tile([P, N // 16], U16, name="offsets")
+        nc.sync.dma_start(offsets[:], offs)
+
+        identity = held.tile([P, P], BF16, name="identity")
+        make_identity(nc, identity[:])
+
+        table_chunks = table.rearrange("(c b p) d -> c p b d", b=BLOCKS, p=P)
+        rows = []
+        for c in range(CHUNKS):
+            rows_c = held.tile([P, BLOCKS, P], BF16, name=f"rows{c}")
+            queue = nc.sync if c % 2 == 0 else nc.scalar
+            queue.dma_start(rows_c[:], table_chunks[c])
+            rows.append(rows_c)
+
+        wq_sb = held.tile([P, P], BF16, name="wq_sb")
+        nc.sync.dma_start(wq_sb[:], wq)
+        bq_sb = held.tile([P, 1], F32, name="bq_sb")
+        nc.sync.dma_start(bq_sb[:], bq)
+        keys_sb = held.tile([P, P], BF16, name="keys_sb")
+        nc.sync.dma_start(keys_sb[:], keys)
+        vals_sb = held.tile([P, P], BF16, name="vals_sb")
+        nc.sync.dma_start(vals_sb[:], vals)
+        bo_sb = held.tile([P, 1], F32, name="bo_sb")
+        nc.sync.dma_start(bo_sb[:], bo)
+        probs_all = held.tile([P, N], F32, name="probs_all")
+        nc.sync.dma_start(probs_all[:], probs.broadcast_to([P, N]))
+
+        keys_temp = held.tile([P, P], BF16, name="keys_temp")
+        nc.vector.tensor_scalar_mul(keys_temp[:], keys_sb[:], TEMP)
+
+        table_t = held.tile([P, S], BF16, name="table_t")
+        for c in range(CHUNKS):
+            table_t_ps = psum.tile([P, PIECE], BF16, name="table_t_ps", tag="flipped")
+            for b in range(BLOCKS):
+                nc.tensor.transpose(table_t_ps[:, b * P : (b + 1) * P], rows[c][:, b, :], identity[:])
+            if c % 2 == 0:
+                nc.vector.tensor_copy(table_t[:, c * PIECE : (c + 1) * PIECE], table_t_ps[:])
+            else:
+                nc.scalar.copy(table_t[:, c * PIECE : (c + 1) * PIECE], table_t_ps[:])
+
+        pieces = range(N // PIECE)
+
+        q_bf = []
+        for h in pieces:
+            q_ps = psum.tile([P, PIECE], F32, name="q_ps")
+            picked = table_t[:].indirect(offsets[:, h * (PIECE // 16) : (h + 1) * (PIECE // 16)])
+            nc.tensor.matmul(q_ps[:], wq_sb[:], picked, start=True, stop=True)
+            q_h = work.tile([P, PIECE], BF16, name="q_h")
+            nc.scalar.activation(q_h[:], q_ps[:], ACT.Identity, bias=bq_sb[:])
+            q_bf.append(q_h)
+
+        att = []
+        for h in pieces:
+            s_ps = psum.tile([P, BLOCKS, P], F32, name="s_ps")
+            for b in range(BLOCKS):
+                nc.tensor.matmul(s_ps[:, b, :], q_bf[h][:, b * P : (b + 1) * P], keys_temp[:], start=True, stop=True)
+            neg_max = work.tile([P, BLOCKS], F32, name="neg_max")
+            nc.vector.tensor_reduce(neg_max[:], s_ps[:], axis=mybir.AxisListType.X, op=ALU.max, negate=True)
+            ex = work.tile([P, BLOCKS, P], F32, name="ex")
+            sums = work.tile([P, BLOCKS], F32, name="sums")
+            for b in range(BLOCKS):
+                nc.scalar.activation(
+                    ex[:, b, :], s_ps[:, b, :], ACT.Exp, bias=neg_max[:, b : b + 1], accum_out=sums[:, b : b + 1]
+                )
+            inv_sums = work.tile([P, BLOCKS], F32, name="inv_sums")
+            nc.vector.reciprocal(inv_sums[:], sums[:])
+            att_h = work.tile([P, BLOCKS, P], BF16, name="att_h")
+            for b in range(BLOCKS):
+                nc.vector.tensor_scalar_mul(att_h[:, b, :], ex[:, b, :], inv_sums[:, b : b + 1])
+            att.append(att_h)
+
+        for h in pieces:
+            att_t_ps = psum.tile([P, PIECE], BF16, name="att_t_ps", tag="flipped")
+            for b in range(BLOCKS):
+                nc.tensor.transpose(att_t_ps[:, b * P : (b + 1) * P], att[h][:, b, :], identity[:])
+            att_t = work.tile([P, PIECE], BF16, name="att_t")
+            nc.scalar.copy(att_t[:], att_t_ps[:])
+            o_ps = psum.tile([P, PIECE], F32, name="o_ps")
+            nc.tensor.matmul(o_ps[:], vals_sb[:], att_t[:], start=True, stop=True)
+            result = work.tile([P, PIECE], F32, name="result")
+            nc.vector.scalar_tensor_tensor(
+                result[:], o_ps[:], bo_sb[:], probs_all[:, h * PIECE : (h + 1) * PIECE], op0=ALU.add, op1=ALU.mult
+            )
+            nc.sync.dma_start(out[:, h * PIECE : (h + 1) * PIECE], result[:])

@@ -8,10 +8,10 @@ ALU = mybir.AluOpType
 P = 128
 S = 2048
 N = 1024
-PIECE = 512
-BLOCKS = PIECE // P
-CHUNKS = S // PIECE
 TEMP = 0.25
+PIECE = 512
+UNIT = 256
+ROWS = PIECE // P
 
 FLOPS = 3 * 2 * P * P * N
 BYTES = N * P * 2 + 3 * P * P * 2 + 2 * P * 4 + N * 4 + P * (N // 16) * 2 + P * N * 4
@@ -19,92 +19,92 @@ BYTES = N * P * 2 + 3 * P * P * 2 + 2 * P * 4 + N * 4 + P * (N // 16) * 2 + P * 
 
 def tile_model_kernel(tc, table, wq, bq, keys, vals, bo, probs, offs, out):
     nc = tc.nc
-    with (
-        tc.tile_pool(name="held", bufs=1) as held,
-        tc.tile_pool(name="work", bufs=2) as work,
-        tc.psum_pool(name="psum", bufs=2) as psum,
-    ):
-        offsets = held.tile([P, N // 16], U16, name="offsets")
-        nc.sync.dma_start(offsets[:], offs)
-
-        identity = held.tile([P, P], BF16, name="identity")
-        make_identity(nc, identity[:])
-
-        table_chunks = table.rearrange("(c b p) d -> c p b d", b=BLOCKS, p=P)
+    with tc.tile_pool(name="held", bufs=1) as held:
+        table_chunks = table.rearrange("(c p r) d -> c p r d", p=P, r=ROWS)
         rows = []
-        for c in range(CHUNKS):
-            rows_c = held.tile([P, BLOCKS, P], BF16, name=f"rows{c}")
+        for c in range(S // PIECE):
+            rows_c = held.tile([P, ROWS, P], BF16, name=f"rows{c}")
             queue = nc.sync if c % 2 == 0 else nc.scalar
             queue.dma_start(rows_c[:], table_chunks[c])
             rows.append(rows_c)
 
+        offsets = held.tile([P, N // 16], U16, name="offsets")
+        nc.sync.dma_start(offsets[:], offs)
         wq_sb = held.tile([P, P], BF16, name="wq_sb")
-        nc.sync.dma_start(wq_sb[:], wq)
+        nc.scalar.dma_start(wq_sb[:], wq)
         bq_sb = held.tile([P, 1], F32, name="bq_sb")
         nc.sync.dma_start(bq_sb[:], bq)
         keys_sb = held.tile([P, P], BF16, name="keys_sb")
-        nc.sync.dma_start(keys_sb[:], keys)
+        nc.scalar.dma_start(keys_sb[:], keys)
         vals_sb = held.tile([P, P], BF16, name="vals_sb")
         nc.sync.dma_start(vals_sb[:], vals)
         bo_sb = held.tile([P, 1], F32, name="bo_sb")
-        nc.sync.dma_start(bo_sb[:], bo)
+        nc.scalar.dma_start(bo_sb[:], bo)
         probs_all = held.tile([P, N], F32, name="probs_all")
         nc.sync.dma_start(probs_all[:], probs.broadcast_to([P, N]))
 
+        identity = held.tile([P, P], BF16, name="identity")
+        make_identity(nc, identity[:])
+
         keys_temp = held.tile([P, P], BF16, name="keys_temp")
-        nc.vector.tensor_scalar_mul(keys_temp[:], keys_sb[:], TEMP)
+        nc.gpsimd.tensor_scalar_mul(keys_temp[:], keys_sb[:], TEMP)
 
         table_t = held.tile([P, S], BF16, name="table_t")
-        for c in range(CHUNKS):
-            table_t_ps = psum.tile([P, PIECE], BF16, name="table_t_ps", tag="flipped")
-            for b in range(BLOCKS):
-                nc.tensor.transpose(table_t_ps[:, b * P : (b + 1) * P], rows[c][:, b, :], identity[:])
-            if c % 2 == 0:
-                nc.vector.tensor_copy(table_t[:, c * PIECE : (c + 1) * PIECE], table_t_ps[:])
-            else:
-                nc.scalar.copy(table_t[:, c * PIECE : (c + 1) * PIECE], table_t_ps[:])
+        with tc.psum_pool(name="table_psum", bufs=4) as table_psum:
+            for c in range(S // PIECE):
+                flipped = table_psum.tile([P, ROWS, P], BF16, name="flipped")
+                for r in range(ROWS):
+                    nc.tensor.transpose(flipped[:, r, :], rows[c][:, r, :], identity[:])
+                in_order = flipped[:].rearrange("d r p -> d p r")
+                window_part = table_t[:, c * PIECE : (c + 1) * PIECE].rearrange("d (p r) -> d p r", r=ROWS)
+                if c % 2 == 0:
+                    nc.vector.tensor_copy(window_part, in_order)
+                else:
+                    nc.scalar.copy(window_part, in_order)
 
-        pieces = range(N // PIECE)
+        with (
+            tc.tile_pool(name="work", bufs=3) as work,
+            tc.psum_pool(name="q_psum", bufs=1) as q_psum,
+            tc.psum_pool(name="psum", bufs=2) as psum,
+        ):
+            q_ps = []
+            for h in range(N // PIECE):
+                q_ps_h = q_psum.tile([P, PIECE], F32, name=f"q_ps{h}")
+                picked = table_t[:].indirect(offsets[:, h * (PIECE // 16) : (h + 1) * (PIECE // 16)])
+                nc.tensor.matmul(q_ps_h[:], wq_sb[:], picked, start=True, stop=True)
+                q_ps.append(q_ps_h)
 
-        q_bf = []
-        for h in pieces:
-            q_ps = psum.tile([P, PIECE], F32, name="q_ps")
-            picked = table_t[:].indirect(offsets[:, h * (PIECE // 16) : (h + 1) * (PIECE // 16)])
-            nc.tensor.matmul(q_ps[:], wq_sb[:], picked, start=True, stop=True)
-            q_h = work.tile([P, PIECE], BF16, name="q_h")
-            nc.scalar.activation(q_h[:], q_ps[:], ACT.Identity, bias=bq_sb[:])
-            q_bf.append(q_h)
+            for u in range(N // UNIT):
+                h, first = divmod(u * UNIT, PIECE)
+                q_bf = work.tile([P, UNIT], BF16, name="q_bf")
+                nc.scalar.activation(q_bf[:], q_ps[h][:, first : first + UNIT], ACT.Identity, bias=bq_sb[:])
 
-        att = []
-        for h in pieces:
-            s_ps = psum.tile([P, BLOCKS, P], F32, name="s_ps")
-            for b in range(BLOCKS):
-                nc.tensor.matmul(s_ps[:, b, :], q_bf[h][:, b * P : (b + 1) * P], keys_temp[:], start=True, stop=True)
-            neg_max = work.tile([P, BLOCKS], F32, name="neg_max")
-            nc.vector.tensor_reduce(neg_max[:], s_ps[:], axis=mybir.AxisListType.X, op=ALU.max, negate=True)
-            ex = work.tile([P, BLOCKS, P], F32, name="ex")
-            sums = work.tile([P, BLOCKS], F32, name="sums")
-            for b in range(BLOCKS):
-                nc.scalar.activation(
-                    ex[:, b, :], s_ps[:, b, :], ACT.Exp, bias=neg_max[:, b : b + 1], accum_out=sums[:, b : b + 1]
+                s_ps = psum.tile([P, UNIT // P, P], F32, name="s_ps")
+                for b in range(UNIT // P):
+                    nc.tensor.matmul(s_ps[:, b, :], q_bf[:, b * P : (b + 1) * P], keys_temp[:], start=True, stop=True)
+                neg_max = work.tile([P, UNIT // P], F32, name="neg_max")
+                nc.vector.tensor_reduce(neg_max[:], s_ps[:], axis=mybir.AxisListType.X, op=ALU.max, negate=True)
+                ex = work.tile([P, UNIT // P, P], F32, name="ex")
+                sums = work.tile([P, UNIT // P], F32, name="sums")
+                for b in range(UNIT // P):
+                    nc.scalar.activation(
+                        ex[:, b, :], s_ps[:, b, :], ACT.Exp, bias=neg_max[:, b : b + 1], accum_out=sums[:, b : b + 1]
+                    )
+                inv_sums = work.tile([P, UNIT // P], F32, name="inv_sums")
+                nc.vector.reciprocal(inv_sums[:], sums[:])
+                att = work.tile([P, UNIT // P, P], BF16, name="att")
+                for b in range(UNIT // P):
+                    nc.vector.tensor_scalar_mul(att[:, b, :], ex[:, b, :], inv_sums[:, b : b + 1])
+
+                att_t_ps = psum.tile([P, UNIT], BF16, name="att_t_ps")
+                for b in range(UNIT // P):
+                    nc.tensor.transpose(att_t_ps[:, b * P : (b + 1) * P], att[:, b, :], identity[:])
+                att_t = work.tile([P, UNIT], BF16, name="att_t")
+                nc.scalar.copy(att_t[:], att_t_ps[:])
+                o_ps = psum.tile([P, UNIT], F32, name="o_ps")
+                nc.tensor.matmul(o_ps[:], vals_sb[:], att_t[:], start=True, stop=True)
+                result = work.tile([P, UNIT], F32, name="result")
+                nc.vector.scalar_tensor_tensor(
+                    result[:], o_ps[:], bo_sb[:], probs_all[:, u * UNIT : (u + 1) * UNIT], op0=ALU.add, op1=ALU.mult
                 )
-            inv_sums = work.tile([P, BLOCKS], F32, name="inv_sums")
-            nc.vector.reciprocal(inv_sums[:], sums[:])
-            att_h = work.tile([P, BLOCKS, P], BF16, name="att_h")
-            for b in range(BLOCKS):
-                nc.vector.tensor_scalar_mul(att_h[:, b, :], ex[:, b, :], inv_sums[:, b : b + 1])
-            att.append(att_h)
-
-        for h in pieces:
-            att_t_ps = psum.tile([P, PIECE], BF16, name="att_t_ps", tag="flipped")
-            for b in range(BLOCKS):
-                nc.tensor.transpose(att_t_ps[:, b * P : (b + 1) * P], att[h][:, b, :], identity[:])
-            att_t = work.tile([P, PIECE], BF16, name="att_t")
-            nc.scalar.copy(att_t[:], att_t_ps[:])
-            o_ps = psum.tile([P, PIECE], F32, name="o_ps")
-            nc.tensor.matmul(o_ps[:], vals_sb[:], att_t[:], start=True, stop=True)
-            result = work.tile([P, PIECE], F32, name="result")
-            nc.vector.scalar_tensor_tensor(
-                result[:], o_ps[:], bo_sb[:], probs_all[:, h * PIECE : (h + 1) * PIECE], op0=ALU.add, op1=ALU.mult
-            )
-            nc.sync.dma_start(out[:, h * PIECE : (h + 1) * PIECE], result[:])
+                nc.sync.dma_start(out[:, u * UNIT : (u + 1) * UNIT], result[:])

@@ -12,6 +12,7 @@ TEMP = 0.25
 PIECE = 512
 UNIT = 256
 ROWS = PIECE // P
+WARM_FIRST = 4
 
 FLOPS = 3 * 2 * P * P * N
 BYTES = N * P * 2 + 3 * P * P * 2 + 2 * P * 4 + N * 4 + P * (N // 16) * 2 + P * N * 4
@@ -49,8 +50,14 @@ def tile_model_kernel(tc, table, wq, bq, keys, vals, bo, probs, offs, out):
         keys_temp = held.tile([P, P], BF16, name="keys_temp")
         nc.gpsimd.tensor_scalar_mul(keys_temp[:], keys_sb[:], TEMP)
 
+        zeros = held.tile([P, PIECE], BF16, name="zeros")
+        nc.vector.memset(zeros[:], 0.0)
+
         table_t = held.tile([P, S], BF16, name="table_t")
-        with tc.psum_pool(name="table_psum", bufs=4) as table_psum:
+        with tc.psum_pool(name="table_psum", bufs=3) as table_psum, tc.psum_pool(name="warm_psum", bufs=1) as warm_psum:
+            unused = warm_psum.tile([P, PIECE], F32, name="unused")
+            for i in range(WARM_FIRST):
+                nc.tensor.matmul(unused[:], zeros[:, :P], zeros[:], start=True, stop=True)
             for c in range(S // PIECE):
                 flipped = table_psum.tile([P, ROWS, P], BF16, name="flipped")
                 for r in range(ROWS):
@@ -61,6 +68,7 @@ def tile_model_kernel(tc, table, wq, bq, keys, vals, bo, probs, offs, out):
                     nc.vector.tensor_copy(window_part, in_order)
                 else:
                     nc.scalar.copy(window_part, in_order)
+                nc.tensor.matmul(unused[:], zeros[:, :P], zeros[:], start=True, stop=True)
 
         with (
             tc.tile_pool(name="work", bufs=3) as work,

@@ -11,8 +11,9 @@ N = 1024
 TEMP = 0.25
 PIECE = 512
 UNIT = 256
+UNITS = N // UNIT
+BLOCKS = UNIT // P
 ROWS = PIECE // P
-WARM_FIRST = 4
 
 FLOPS = 3 * 2 * P * P * N
 BYTES = N * P * 2 + 3 * P * P * 2 + 2 * P * 4 + N * 4 + P * (N // 16) * 2 + P * N * 4
@@ -50,14 +51,8 @@ def tile_model_kernel(tc, table, wq, bq, keys, vals, bo, probs, offs, out):
         keys_temp = held.tile([P, P], BF16, name="keys_temp")
         nc.gpsimd.tensor_scalar_mul(keys_temp[:], keys_sb[:], TEMP)
 
-        zeros = held.tile([P, PIECE], BF16, name="zeros")
-        nc.vector.memset(zeros[:], 0.0)
-
         table_t = held.tile([P, S], BF16, name="table_t")
-        with tc.psum_pool(name="table_psum", bufs=3) as table_psum, tc.psum_pool(name="warm_psum", bufs=1) as warm_psum:
-            unused = warm_psum.tile([P, PIECE], F32, name="unused")
-            for i in range(WARM_FIRST):
-                nc.tensor.matmul(unused[:], zeros[:, :P], zeros[:], start=True, stop=True)
+        with tc.psum_pool(name="table_psum", bufs=4) as table_psum:
             for c in range(S // PIECE):
                 flipped = table_psum.tile([P, ROWS, P], BF16, name="flipped")
                 for r in range(ROWS):
@@ -68,51 +63,52 @@ def tile_model_kernel(tc, table, wq, bq, keys, vals, bo, probs, offs, out):
                     nc.vector.tensor_copy(window_part, in_order)
                 else:
                     nc.scalar.copy(window_part, in_order)
-                nc.tensor.matmul(unused[:], zeros[:, :P], zeros[:], start=True, stop=True)
 
-        with (
-            tc.tile_pool(name="work", bufs=3) as work,
-            tc.psum_pool(name="q_psum", bufs=1) as q_psum,
-            tc.psum_pool(name="psum", bufs=2) as psum,
-        ):
-            q_ps = []
-            for h in range(N // PIECE):
-                q_ps_h = q_psum.tile([P, PIECE], F32, name=f"q_ps{h}")
-                picked = table_t[:].indirect(offsets[:, h * (PIECE // 16) : (h + 1) * (PIECE // 16)])
-                nc.tensor.matmul(q_ps_h[:], wq_sb[:], picked, start=True, stop=True)
-                q_ps.append(q_ps_h)
+        with tc.tile_pool(name="work", bufs=UNITS) as work, tc.psum_pool(name="s_psum", bufs=UNITS) as s_psum:
+            q_bf = []
+            with tc.psum_pool(name="q_psum", bufs=1) as q_psum:
+                q_ps = []
+                for h in range(N // PIECE):
+                    q_ps_h = q_psum.tile([P, PIECE], F32, name=f"q_ps{h}")
+                    picked = table_t[:].indirect(offsets[:, h * (PIECE // 16) : (h + 1) * (PIECE // 16)])
+                    nc.tensor.matmul(q_ps_h[:], wq_sb[:], picked, start=True, stop=True)
+                    q_ps.append(q_ps_h)
+                for u in range(UNITS):
+                    h, first = divmod(u * UNIT, PIECE)
+                    q_u = work.tile([P, UNIT], BF16, name="q_u")
+                    nc.scalar.activation(q_u[:], q_ps[h][:, first : first + UNIT], ACT.Identity, bias=bq_sb[:])
+                    q_bf.append(q_u)
 
-            for u in range(N // UNIT):
-                h, first = divmod(u * UNIT, PIECE)
-                q_bf = work.tile([P, UNIT], BF16, name="q_bf")
-                nc.scalar.activation(q_bf[:], q_ps[h][:, first : first + UNIT], ACT.Identity, bias=bq_sb[:])
+            with tc.psum_pool(name="late_psum", bufs=2) as late_psum:
+                for u in range(UNITS):
+                    s_ps = s_psum.tile([P, BLOCKS, P], F32, name="s_ps")
+                    for b in range(BLOCKS):
+                        nc.tensor.matmul(
+                            s_ps[:, b, :], q_bf[u][:, b * P : (b + 1) * P], keys_temp[:], start=True, stop=True
+                        )
+                    neg_max = work.tile([P, BLOCKS], F32, name="neg_max")
+                    nc.vector.tensor_reduce(neg_max[:], s_ps[:], axis=mybir.AxisListType.X, op=ALU.max, negate=True)
+                    ex = work.tile([P, BLOCKS, P], F32, name="ex")
+                    sums = work.tile([P, BLOCKS], F32, name="sums")
+                    for b in range(BLOCKS):
+                        nc.scalar.activation(
+                            ex[:, b, :], s_ps[:, b, :], ACT.Exp, bias=neg_max[:, b : b + 1], accum_out=sums[:, b : b + 1]
+                        )
+                    inv_sums = work.tile([P, BLOCKS], F32, name="inv_sums")
+                    nc.vector.reciprocal(inv_sums[:], sums[:])
+                    att = work.tile([P, BLOCKS, P], BF16, name="att")
+                    for b in range(BLOCKS):
+                        nc.vector.tensor_scalar_mul(att[:, b, :], ex[:, b, :], inv_sums[:, b : b + 1])
 
-                s_ps = psum.tile([P, UNIT // P, P], F32, name="s_ps")
-                for b in range(UNIT // P):
-                    nc.tensor.matmul(s_ps[:, b, :], q_bf[:, b * P : (b + 1) * P], keys_temp[:], start=True, stop=True)
-                neg_max = work.tile([P, UNIT // P], F32, name="neg_max")
-                nc.vector.tensor_reduce(neg_max[:], s_ps[:], axis=mybir.AxisListType.X, op=ALU.max, negate=True)
-                ex = work.tile([P, UNIT // P, P], F32, name="ex")
-                sums = work.tile([P, UNIT // P], F32, name="sums")
-                for b in range(UNIT // P):
-                    nc.scalar.activation(
-                        ex[:, b, :], s_ps[:, b, :], ACT.Exp, bias=neg_max[:, b : b + 1], accum_out=sums[:, b : b + 1]
+                    att_t_ps = late_psum.tile([P, UNIT], BF16, name="att_t_ps")
+                    for b in range(BLOCKS):
+                        nc.tensor.transpose(att_t_ps[:, b * P : (b + 1) * P], att[:, b, :], identity[:])
+                    att_t = work.tile([P, UNIT], BF16, name="att_t")
+                    nc.scalar.copy(att_t[:], att_t_ps[:])
+                    o_ps = late_psum.tile([P, UNIT], F32, name="o_ps")
+                    nc.tensor.matmul(o_ps[:], vals_sb[:], att_t[:], start=True, stop=True)
+                    result = work.tile([P, UNIT], F32, name="result")
+                    nc.vector.scalar_tensor_tensor(
+                        result[:], o_ps[:], bo_sb[:], probs_all[:, u * UNIT : (u + 1) * UNIT], op0=ALU.add, op1=ALU.mult
                     )
-                inv_sums = work.tile([P, UNIT // P], F32, name="inv_sums")
-                nc.vector.reciprocal(inv_sums[:], sums[:])
-                att = work.tile([P, UNIT // P, P], BF16, name="att")
-                for b in range(UNIT // P):
-                    nc.vector.tensor_scalar_mul(att[:, b, :], ex[:, b, :], inv_sums[:, b : b + 1])
-
-                att_t_ps = psum.tile([P, UNIT], BF16, name="att_t_ps")
-                for b in range(UNIT // P):
-                    nc.tensor.transpose(att_t_ps[:, b * P : (b + 1) * P], att[:, b, :], identity[:])
-                att_t = work.tile([P, UNIT], BF16, name="att_t")
-                nc.scalar.copy(att_t[:], att_t_ps[:])
-                o_ps = psum.tile([P, UNIT], F32, name="o_ps")
-                nc.tensor.matmul(o_ps[:], vals_sb[:], att_t[:], start=True, stop=True)
-                result = work.tile([P, UNIT], F32, name="result")
-                nc.vector.scalar_tensor_tensor(
-                    result[:], o_ps[:], bo_sb[:], probs_all[:, u * UNIT : (u + 1) * UNIT], op0=ALU.add, op1=ALU.mult
-                )
-                nc.sync.dma_start(out[:, u * UNIT : (u + 1) * UNIT], result[:])
+                    nc.sync.dma_start(out[:, u * UNIT : (u + 1) * UNIT], result[:])

import concourse.mybir as mybir
from concourse.masks import make_identity

BF16, F32, U16 = mybir.dt.bfloat16, mybir.dt.float32, mybir.dt.uint16
ACT = mybir.ActivationFunctionType
ALU = mybir.AluOpType

P = 128
S = 2048
N = 1024
TEMP = 0.25
PIECE = 512
UNIT = 256
UNITS = N // UNIT
BLOCKS = UNIT // P
ROWS = PIECE // P

FLOPS = 3 * 2 * P * P * N
BYTES = N * P * 2 + 3 * P * P * 2 + 2 * P * 4 + N * 4 + P * (N // 16) * 2 + P * N * 4


def tile_model_kernel(tc, table, wq, bq, keys, vals, bo, probs, offs, out):
    nc = tc.nc
    with tc.tile_pool(name="held", bufs=1) as held:
        table_chunks = table.rearrange("(c p r) d -> c p r d", p=P, r=ROWS)
        rows = []
        for c in range(S // PIECE):
            rows_c = held.tile([P, ROWS, P], BF16, name=f"rows{c}")
            queue = nc.sync if c % 2 == 0 else nc.scalar
            queue.dma_start(rows_c[:], table_chunks[c])
            rows.append(rows_c)

        offsets = held.tile([P, N // 16], U16, name="offsets")
        nc.sync.dma_start(offsets[:], offs)
        wq_sb = held.tile([P, P], BF16, name="wq_sb")
        nc.scalar.dma_start(wq_sb[:], wq)
        bq_sb = held.tile([P, 1], F32, name="bq_sb")
        nc.sync.dma_start(bq_sb[:], bq)
        keys_sb = held.tile([P, P], BF16, name="keys_sb")
        nc.scalar.dma_start(keys_sb[:], keys)
        vals_sb = held.tile([P, P], BF16, name="vals_sb")
        nc.sync.dma_start(vals_sb[:], vals)
        bo_sb = held.tile([P, 1], F32, name="bo_sb")
        nc.scalar.dma_start(bo_sb[:], bo)
        probs_all = held.tile([P, N], F32, name="probs_all")
        nc.sync.dma_start(probs_all[:], probs.broadcast_to([P, N]))

        identity = held.tile([P, P], BF16, name="identity")
        make_identity(nc, identity[:])

        keys_temp = held.tile([P, P], BF16, name="keys_temp")
        nc.gpsimd.tensor_scalar_mul(keys_temp[:], keys_sb[:], TEMP)

        table_t = held.tile([P, S], BF16, name="table_t")
        with tc.psum_pool(name="table_psum", bufs=4) as table_psum:
            for c in range(S // PIECE):
                flipped = table_psum.tile([P, ROWS, P], BF16, name="flipped")
                for r in range(ROWS):
                    nc.tensor.transpose(flipped[:, r, :], rows[c][:, r, :], identity[:])
                in_order = flipped[:].rearrange("d r p -> d p r")
                window_part = table_t[:, c * PIECE : (c + 1) * PIECE].rearrange("d (p r) -> d p r", r=ROWS)
                if c % 2 == 0:
                    nc.vector.tensor_copy(window_part, in_order)
                else:
                    nc.scalar.copy(window_part, in_order)

        with tc.tile_pool(name="work", bufs=UNITS) as work, tc.psum_pool(name="s_psum", bufs=UNITS) as s_psum:
            q_bf = []
            with tc.psum_pool(name="q_psum", bufs=1) as q_psum:
                q_ps = []
                for h in range(N // PIECE):
                    q_ps_h = q_psum.tile([P, PIECE], F32, name=f"q_ps{h}")
                    picked = table_t[:].indirect(offsets[:, h * (PIECE // 16) : (h + 1) * (PIECE // 16)])
                    nc.tensor.matmul(q_ps_h[:], wq_sb[:], picked, start=True, stop=True)
                    q_ps.append(q_ps_h)
                for u in range(UNITS):
                    h, first = divmod(u * UNIT, PIECE)
                    q_u = work.tile([P, UNIT], BF16, name="q_u")
                    nc.scalar.activation(q_u[:], q_ps[h][:, first : first + UNIT], ACT.Identity, bias=bq_sb[:])
                    q_bf.append(q_u)

            with tc.psum_pool(name="late_psum", bufs=2) as late_psum:
                for u in range(UNITS):
                    s_ps = s_psum.tile([P, BLOCKS, P], F32, name="s_ps")
                    for b in range(BLOCKS):
                        nc.tensor.matmul(
                            s_ps[:, b, :], q_bf[u][:, b * P : (b + 1) * P], keys_temp[:], start=True, stop=True
                        )
                    neg_max = work.tile([P, BLOCKS], F32, name="neg_max")
                    nc.vector.tensor_reduce(neg_max[:], s_ps[:], axis=mybir.AxisListType.X, op=ALU.max, negate=True)
                    ex = work.tile([P, BLOCKS, P], F32, name="ex")
                    sums = work.tile([P, BLOCKS], F32, name="sums")
                    for b in range(BLOCKS):
                        nc.scalar.activation(
                            ex[:, b, :], s_ps[:, b, :], ACT.Exp, bias=neg_max[:, b : b + 1], accum_out=sums[:, b : b + 1]
                        )
                    inv_sums = work.tile([P, BLOCKS], F32, name="inv_sums")
                    nc.vector.reciprocal(inv_sums[:], sums[:])
                    att = work.tile([P, BLOCKS, P], BF16, name="att")
                    for b in range(BLOCKS):
                        nc.vector.tensor_scalar_mul(att[:, b, :], ex[:, b, :], inv_sums[:, b : b + 1])

                    att_t_ps = late_psum.tile([P, UNIT], BF16, name="att_t_ps")
                    for b in range(BLOCKS):
                        nc.tensor.transpose(att_t_ps[:, b * P : (b + 1) * P], att[:, b, :], identity[:])
                    att_t = work.tile([P, UNIT], BF16, name="att_t")
                    nc.scalar.copy(att_t[:], att_t_ps[:])
                    o_ps = late_psum.tile([P, UNIT], F32, name="o_ps")
                    nc.tensor.matmul(o_ps[:], vals_sb[:], att_t[:], start=True, stop=True)
                    result = work.tile([P, UNIT], F32, name="result")
                    nc.vector.scalar_tensor_tensor(
                        result[:], o_ps[:], bo_sb[:], probs_all[:, u * UNIT : (u + 1) * UNIT], op0=ALU.add, op1=ALU.mult
                    )
                    nc.sync.dma_start(out[:, u * UNIT : (u + 1) * UNIT], result[:])
